import numpy as np
import ml_dtypes


def mxq(x, axis, fmt="e4m3"):
    dtype, down = {"e4m3": (ml_dtypes.float8_e4m3fn, 7), "e5m2": (ml_dtypes.float8_e5m2, 14)}[fmt]
    v = np.moveaxis(np.asarray(x, np.float32).astype(ml_dtypes.bfloat16).astype(np.float64), axis, -1)
    blocks = v.reshape(v.shape[:-1] + (-1, 32))
    amax = np.abs(blocks).max(-1, keepdims=True)
    byte = np.maximum(np.where(amax > 0, np.frexp(amax)[1] - 1 + 127, 0) - down, 1)
    scale = np.exp2(byte - 127.0)
    codes = (blocks / scale).astype(np.float32).astype(dtype).astype(np.float64)
    return np.moveaxis((codes * scale).reshape(v.shape), -1, axis)


WIDE = False


def mx_kscale(k):
    if not WIDE:
        return np.ones(k)
    levels = np.array([10, -10, 5, -5, 0])
    a = np.random.permutation(np.resize(levels, k // 512 * 4)).reshape(k // 512, 4)
    idx = np.arange(k)
    return np.exp2(a[idx // 512, idx % 128 // 32])


BF16 = ml_dtypes.bfloat16


def bf(x):
    return np.asarray(x, np.float32).astype(BF16)


def f64(x):
    return np.asarray(x).astype(np.float64)


B, S, C, H, D = 4, 512, 1024, 8, 128
E = H * D
EPS = 1e-15


def setup_inputs():
    t = mx_kscale(E)
    return {"q_feat": bf(np.maximum(np.random.standard_normal((B, H, S, D)), 0.0)),
            "vk": bf(np.random.standard_normal((B, H, D, D)) * np.sqrt(S) * t.reshape(H, D)[None, :, :, None]),
            "k_sum": bf(S * (0.11 + 0.02 * np.random.standard_normal((B, H, D)))),
            "Wo": bf(np.random.standard_normal((C, E)) * 6.0 / np.sqrt(E) / t[None, :]),
            "bo": bf(np.random.standard_normal(C) * 0.1)}


def reference(q_feat, vk, k_sum, Wo, bo):
    hs = f64(vk) @ f64(q_feat).transpose(0, 1, 3, 2)
    den = (f64(q_feat) * f64(k_sum)[:, :, None, :]).sum(-1)
    hs = hs / (den[:, :, None, :] + EPS)
    a = hs.transpose(0, 3, 1, 2).reshape(B, S, E)
    return (mxq(a, 2, "e4m3") @ mxq(f64(Wo), 1, "e4m3").T) + f64(bo)

@@ -1,0 +1,235 @@
+from contextlib import ExitStack
+
+import concourse.mybir as mybir
+from concourse.masks import make_identity
+
+BF16 = mybir.dt.bfloat16
+F32 = mybir.dt.float32
+U32 = mybir.dt.uint32
+U8 = mybir.dt.uint8
+FP8X4 = mybir.dt.float8_e4m3fn_x4
+COPY = mybir.ActivationFunctionType.Copy
+ADD = mybir.AluOpType.add
+
+B, H, S, D, C = 4, 8, 512, 128, 1024
+E = H * D
+EPS = 1e-15
+P = 128
+PACK = 4
+K_PASS = P * PACK
+PASSES = E // K_PASS
+BANK = 512
+CHUNKS = S // P
+UNITS = B * CHUNKS
+C_HALVES = C // BANK
+READ = D + 1
+HEADS_PER_BANK = BANK // READ
+HS_BANKS = -(-H // HEADS_PER_BANK)
+VK_SLOT = 144
+
+FLOPS = 2 * B * S * E * C + 2 * B * H * S * D * (D + 1)
+
+
+def tile_lineartransformerblock_pc_kernel(tc, q_feat, vk, k_sum, Wo, bo, out):
+    nc = tc.nc
+    with ExitStack() as ctx:
+        ctx.enter_context(tc.manual_schedule())
+        keep = ctx.enter_context(tc.tile_pool(name="keep", bufs=1))
+        work = ctx.enter_context(tc.tile_pool(name="work", bufs=3))
+        psum = ctx.enter_context(tc.psum_pool(name="psum", bufs=1))
+
+        vk_sb = []
+        q_sb = []
+        for b in range(B):
+            vk_b = keep.tile([P, H, D], BF16, name="vk%d" % b)
+            q_b = keep.tile([P, H, CHUNKS * D], BF16, name="q%d" % b)
+            vk_sb.append(vk_b)
+            q_sb.append(q_b)
+        wo_sb = keep.tile([P, C // P, E], BF16)
+
+        def load_batch(b):
+            nc.sync.dma_start(out=vk_sb[b][:], in_=vk[b].rearrange("h n d -> n h d"))
+            nc.sync.dma_start(out=q_sb[b][:], in_=q_feat[b].rearrange("h (p j) d -> p h (j d)", j=CHUNKS))
+
+        ks_rows = keep.tile([P, D], BF16)
+        nc.sync.dma_start(out=ks_rows[0 : B * H, :], in_=k_sum.rearrange("b h d -> (b h) d"))
+        nc.vector.memset(ks_rows[32:64, :], 0.0)
+        nc.vector.memset(ks_rows[64:128, :], 0.0)
+        bo_rows = keep.tile([P, C], BF16)
+        nc.vector.memset(bo_rows[:], 0.0)
+
+        wo_rows = Wo.rearrange("(k p) e -> p k e", p=P)
+        load_batch(0)
+        nc.sync.dma_start(out=bo_rows[0:1, :], in_=bo.rearrange("(o c) -> o c", o=1))
+        for half in range(C_HALVES):
+            rows = slice(half * (BANK // P), (half + 1) * (BANK // P))
+            nc.sync.dma_start(out=wo_sb[:, rows, :], in_=wo_rows[:, rows, :])
+        for b in range(1, B):
+            load_batch(b)
+
+        ident_bf = keep.tile([P, P], BF16)
+        make_identity(nc, ident_bf[:])
+        ident_f32 = keep.tile([P, P], F32)
+        make_identity(nc, ident_f32[:])
+        ones = keep.tile([P, P], BF16)
+        nc.vector.memset(ones[:], 1.0)
+
+        bias = keep.tile([P, C], F32)
+
+        def spread_bias():
+            for half in range(C_HALVES):
+                cols = slice(half * BANK, (half + 1) * BANK)
+                spread = psum.tile([P, BANK], F32, tag="acc", bufs=3)
+                nc.tensor.matmul(out=spread[:], lhsT=ones[:], rhs=bo_rows[:, cols], start=True, stop=True)
+                nc.vector.tensor_copy(out=bias[:, cols], in_=spread[:])
+
+        vkT = keep.tile([P, B * H, VK_SLOT], BF16)
+        ksT = psum.tile([P, P], BF16, tag="tq")
+        nc.tensor.transpose(ksT[:], ks_rows[:], ident_bf[:])
+        nc.vector.tensor_copy(out=vkT[:, :, D : D + 1], in_=ksT[:, 0 : B * H].unsqueeze(2))
+
+        def transpose_vk(b):
+            flipped = psum.tile([P, H, D], BF16, tag="acc", bufs=3)
+            for h in range(H):
+                nc.tensor.transpose(flipped[:, h, :], vk_sb[b][:, h, :], ident_bf[:])
+            nc.vector.tensor_copy(out=vkT[:, b * H : (b + 1) * H, 0:D], in_=flipped[:])
+
+        wo_words = wo_sb[:].rearrange("p k e -> p (k e)").bitcast(F32)
+        wo_grouped = keep.tile([P, PASSES * C * PACK], BF16, align_bytes=64)
+        wo_pairs = wo_grouped[:].bitcast(F32).rearrange("p (g c u) -> p g c u", g=PASSES, u=2)
+        wo_codes = keep.tile([P, PASSES * C], U32, align_bytes=64)
+        wo_scales = keep.tile([P, PASSES * C], U8, align_bytes=64)
+
+        def prepare_wo():
+            for half in range(C_HALVES):
+                for g in range(PASSES):
+                    for quarter in range(2):
+                        c0 = half * BANK + quarter * 2 * P
+                        flipped = psum.tile([P, 2, 2 * P], F32, tag="acc", bufs=3)
+                        for u in range(2):
+                            for k in range(2):
+                                first = (c0 // P + k) * (E // 2) + (2 * g + u) * P
+                                nc.tensor.transpose(
+                                    flipped[:, u, k * P : (k + 1) * P], wo_words[:, first : first + P], ident_f32[:]
+                                )
+                        pairs = wo_pairs[:, g, c0 : c0 + 2 * P, :]
+                        if quarter == 0:
+                            nc.scalar.copy(out=pairs, in_=flipped[:].rearrange("p u c -> p c u"))
+                        else:
+                            nc.vector.tensor_copy(out=pairs, in_=flipped[:].rearrange("p u c -> p c u"))
+                    first = g * C + half * BANK
+                    nc.vector.quantize_mx(
+                        out=wo_codes[:, first : first + BANK].bitcast(FP8X4),
+                        scales=wo_scales[:, first : first + BANK],
+                        in_=wo_grouped[:, first * PACK : (first + BANK) * PACK],
+                    )
+
+        qT = {}
+        a_rows = {}
+        a_grouped = {}
+        a_codes = {}
+        a_scales = {}
+
+        def transpose_q(u):
+            b, j = divmod(u, CHUNKS)
+            flipped = psum.tile([P, H, P], BF16, tag="tq")
+            for h in range(H):
+                nc.tensor.transpose(flipped[:, h, :], q_sb[b][:, h, j * D : (j + 1) * D], ident_bf[:])
+            qT_u = work.tile([P, H, P], BF16, tag="qT")
+            nc.scalar.copy(out=qT_u[:], in_=flipped[:])
+            qT[u] = qT_u
+
+        def read_out(u):
+            b = u // CHUNKS
+            banks = []
+            for k in range(HS_BANKS):
+                bank = psum.tile([P, BANK], F32, tag="hs%d" % k)
+                banks.append(bank)
+            for h in range(H):
+                k, slot = divmod(h, HEADS_PER_BANK)
+                nc.tensor.matmul(
+                    out=banks[k][:, slot * READ : (slot + 1) * READ],
+                    lhsT=qT[u][:, h, :],
+                    rhs=vkT[:, b * H + h, 0:READ],
+                    start=True,
+                    stop=True,
+                )
+            den = work.tile([P, H], F32, tag="den")
+            for k in range(HS_BANKS):
+                h0 = k * HEADS_PER_BANK
+                n = min(HEADS_PER_BANK, H - h0)
+                slots = banks[k][:, 0 : n * READ].rearrange("p (k r) -> p k r", r=READ)
+                nc.vector.tensor_scalar_add(out=den[:, h0 : h0 + n].unsqueeze(2), in0=slots[:, :, D:READ], scalar1=EPS)
+            rden = work.tile([P, H], F32, tag="rden")
+            nc.vector.reciprocal(out=rden[:], in_=den[:])
+            a_u = work.tile([P, E], BF16, tag="a")
+            for h in range(H):
+                k, slot = divmod(h, HEADS_PER_BANK)
+                nc.scalar.activation(
+                    out=a_u[:, h * D : (h + 1) * D],
+                    in_=banks[k][:, slot * READ : slot * READ + D],
+                    func=COPY,
+                    scale=rden[:, h : h + 1],
+                )
+            a_rows[u] = a_u
+
+        def transpose_a(u):
+            words = a_rows[u][:].bitcast(F32)
+            flipped = psum.tile([P, BANK], F32, tag="ta")
+            for w in range(E // 2 // P):
+                nc.tensor.transpose(flipped[:, w * P : (w + 1) * P], words[:, w * P : (w + 1) * P], ident_f32[:])
+            grouped = work.tile([P, E], BF16, tag="grouped", align_bytes=64)
+            nc.scalar.copy(
+                out=grouped[:].bitcast(F32).rearrange("p (g s u) -> p g s u", g=PASSES, u=2),
+                in_=flipped[:].rearrange("p (g u s) -> p g s u", g=PASSES, u=2),
+            )
+            a_grouped[u] = grouped
+
+        def quantise_a(u):
+            codes = work.tile([P, PASSES * P], U32, tag="codes", bufs=4, align_bytes=64)
+            scales = work.tile([P, PASSES * P], U8, tag="scales", bufs=4, align_bytes=64)
+            nc.vector.quantize_mx(out=codes[:].bitcast(FP8X4), scales=scales[:], in_=a_grouped[u][:])
+            a_codes[u] = codes
+            a_scales[u] = scales
+
+        def project(u):
+            b, j = divmod(u, CHUNKS)
+            rows = out[b].rearrange("(p j) c -> p j c", j=CHUNKS)
+            for half in range(C_HALVES):
+                acc = psum.tile([P, BANK], F32, tag="acc", bufs=3)
+                for g in range(PASSES):
+                    tokens = slice(g * P, (g + 1) * P)
+                    cols = slice(g * C + half * BANK, g * C + (half + 1) * BANK)
+                    nc.tensor.matmul_mx(
+                        out=acc[:],
+                        lhsT=a_codes[u][:, tokens].bitcast(FP8X4),
+                        lhsT_scale=a_scales[u][:, tokens],
+                        rhs=wo_codes[:, cols].bitcast(FP8X4),
+                        rhs_scale=wo_scales[:, cols],
+                        start=(g == 0),
+                        stop=(g == PASSES - 1),
+                    )
+                cols = slice(half * BANK, (half + 1) * BANK)
+                res = work.tile([P, BANK], F32, tag="res", bufs=6)
+                nc.vector.tensor_tensor(out=res[:], in0=acc[:], in1=bias[:, cols], op=ADD)
+                nc.sync.dma_start(out=rows[:, j, cols], in_=res[:])
+
+        READ_LAG = 1
+        FLIP_LAG = 3
+        PROJECT_LAG = 5
+        for t in range(UNITS + PROJECT_LAG):
+            if t < UNITS and t % CHUNKS == 0:
+                transpose_vk(t // CHUNKS)
+            if t == CHUNKS:
+                spread_bias()
+                prepare_wo()
+            if t < UNITS:
+                transpose_q(t)
+            if 0 <= t - FLIP_LAG < UNITS:
+                transpose_a(t - FLIP_LAG)
+            if 0 <= t - READ_LAG < UNITS:
+                read_out(t - READ_LAG)
+            if 0 <= t - FLIP_LAG < UNITS:
+                quantise_a(t - FLIP_LAG)
+            if 0 <= t - PROJECT_LAG < UNITS:
+                project(t - PROJECT_LAG)

@@ -10,6 +10,7 @@ U8 = mybir.dt.uint8
 FP8X4 = mybir.dt.float8_e4m3fn_x4
 COPY = mybir.ActivationFunctionType.Copy
 ADD = mybir.AluOpType.add
+MULT = mybir.AluOpType.mult
 
 B, H, S, D, C = 4, 8, 512, 128, 1024
 E = H * D
@@ -163,7 +164,14 @@ def tile_lineartransformerblock_pc_kernel(tc, q_feat, vk, k_sum, Wo, bo, out):
             rden = work.tile([P, H], F32, tag="rden")
             nc.vector.reciprocal(out=rden[:], in_=den[:])
             a_u = work.tile([P, E], BF16, tag="a")
-            for h in range(H):
+            first_heads = banks[0][:, 0 : HEADS_PER_BANK * READ].rearrange("p (k r) -> p k r", r=READ)
+            nc.vector.tensor_tensor(
+                out=a_u[:, 0 : HEADS_PER_BANK * D].rearrange("p (k n) -> p k n", n=D),
+                in0=first_heads[:, :, 0:D],
+                in1=rden[:, 0:HEADS_PER_BANK].unsqueeze(2).to_broadcast([P, HEADS_PER_BANK, D]),
+                op=MULT,
+            )
+            for h in range(HEADS_PER_BANK, H):
                 k, slot = divmod(h, HEADS_PER_BANK)
                 nc.scalar.activation(
                     out=a_u[:, h * D : (h + 1) * D],

@@ -37,7 +37,7 @@ def tile_lineartransformerblock_pc_kernel(tc, q_feat, vk, k_sum, Wo, bo, out):
         ctx.enter_context(tc.manual_schedule())
         keep = ctx.enter_context(tc.tile_pool(name="keep", bufs=1))
         work = ctx.enter_context(tc.tile_pool(name="work", bufs=3))
-        psum = ctx.enter_context(tc.psum_pool(name="psum", bufs=1))
+        psum = ctx.enter_context(tc.psum_pool(name="psum", bufs=8))
 
         vk_sb = []
         q_sb = []
@@ -80,17 +80,17 @@ def tile_lineartransformerblock_pc_kernel(tc, q_feat, vk, k_sum, Wo, bo, out):
         def spread_bias():
             for half in range(C_HALVES):
                 cols = slice(half * BANK, (half + 1) * BANK)
-                spread = psum.tile([P, BANK], F32, tag="acc", bufs=3)
+                spread = psum.tile([P, BANK], F32, tag="bank")
                 nc.tensor.matmul(out=spread[:], lhsT=ones[:], rhs=bo_rows[:, cols], start=True, stop=True)
                 nc.vector.tensor_copy(out=bias[:, cols], in_=spread[:])
 
         vkT = keep.tile([P, B * H, VK_SLOT], BF16)
-        ksT = psum.tile([P, P], BF16, tag="tq")
+        ksT = psum.tile([P, P], BF16, tag="bank")
         nc.tensor.transpose(ksT[:], ks_rows[:], ident_bf[:])
         nc.vector.tensor_copy(out=vkT[:, :, D : D + 1], in_=ksT[:, 0 : B * H].unsqueeze(2))
 
         def transpose_vk(b):
-            flipped = psum.tile([P, H, D], BF16, tag="acc", bufs=3)
+            flipped = psum.tile([P, H, D], BF16, tag="bank")
             for h in range(H):
                 nc.tensor.transpose(flipped[:, h, :], vk_sb[b][:, h, :], ident_bf[:])
             nc.vector.tensor_copy(out=vkT[:, b * H : (b + 1) * H, 0:D], in_=flipped[:])
@@ -101,29 +101,27 @@ def tile_lineartransformerblock_pc_kernel(tc, q_feat, vk, k_sum, Wo, bo, out):
         wo_codes = keep.tile([P, PASSES * C], U32, align_bytes=64)
         wo_scales = keep.tile([P, PASSES * C], U8, align_bytes=64)
 
-        def prepare_wo():
-            for half in range(C_HALVES):
-                for g in range(PASSES):
-                    for quarter in range(2):
-                        c0 = half * BANK + quarter * 2 * P
-                        flipped = psum.tile([P, 2, 2 * P], F32, tag="acc", bufs=3)
-                        for u in range(2):
-                            for k in range(2):
-                                first = (c0 // P + k) * (E // 2) + (2 * g + u) * P
-                                nc.tensor.transpose(
-                                    flipped[:, u, k * P : (k + 1) * P], wo_words[:, first : first + P], ident_f32[:]
-                                )
-                        pairs = wo_pairs[:, g, c0 : c0 + 2 * P, :]
-                        if quarter == 0:
-                            nc.scalar.copy(out=pairs, in_=flipped[:].rearrange("p u c -> p c u"))
-                        else:
-                            nc.vector.tensor_copy(out=pairs, in_=flipped[:].rearrange("p u c -> p c u"))
-                    first = g * C + half * BANK
-                    nc.vector.quantize_mx(
-                        out=wo_codes[:, first : first + BANK].bitcast(FP8X4),
-                        scales=wo_scales[:, first : first + BANK],
-                        in_=wo_grouped[:, first * PACK : (first + BANK) * PACK],
-                    )
+        def prepare_wo(half, g):
+            for quarter in range(2):
+                c0 = half * BANK + quarter * 2 * P
+                flipped = psum.tile([P, 2, 2 * P], F32, tag="bank")
+                for u in range(2):
+                    for k in range(2):
+                        first = (c0 // P + k) * (E // 2) + (2 * g + u) * P
+                        nc.tensor.transpose(
+                            flipped[:, u, k * P : (k + 1) * P], wo_words[:, first : first + P], ident_f32[:]
+                        )
+                pairs = wo_pairs[:, g, c0 : c0 + 2 * P, :]
+                if quarter == 0:
+                    nc.scalar.copy(out=pairs, in_=flipped[:].rearrange("p u c -> p c u"))
+                else:
+                    nc.vector.tensor_copy(out=pairs, in_=flipped[:].rearrange("p u c -> p c u"))
+            first = g * C + half * BANK
+            nc.vector.quantize_mx(
+                out=wo_codes[:, first : first + BANK].bitcast(FP8X4),
+                scales=wo_scales[:, first : first + BANK],
+                in_=wo_grouped[:, first * PACK : (first + BANK) * PACK],
+            )
 
         qT = {}
         a_rows = {}
@@ -133,7 +131,7 @@ def tile_lineartransformerblock_pc_kernel(tc, q_feat, vk, k_sum, Wo, bo, out):
 
         def transpose_q(u):
             b, j = divmod(u, CHUNKS)
-            flipped = psum.tile([P, H, P], BF16, tag="tq")
+            flipped = psum.tile([P, H, P], BF16, tag="bank")
             for h in range(H):
                 nc.tensor.transpose(flipped[:, h, :], q_sb[b][:, h, j * D : (j + 1) * D], ident_bf[:])
             qT_u = work.tile([P, H, P], BF16, tag="qT")
@@ -144,7 +142,7 @@ def tile_lineartransformerblock_pc_kernel(tc, q_feat, vk, k_sum, Wo, bo, out):
             b = u // CHUNKS
             banks = []
             for k in range(HS_BANKS):
-                bank = psum.tile([P, BANK], F32, tag="hs%d" % k)
+                bank = psum.tile([P, BANK], F32, tag="bank")
                 banks.append(bank)
             for h in range(H):
                 k, slot = divmod(h, HEADS_PER_BANK)
@@ -183,7 +181,7 @@ def tile_lineartransformerblock_pc_kernel(tc, q_feat, vk, k_sum, Wo, bo, out):
 
         def transpose_a(u):
             words = a_rows[u][:].bitcast(F32)
-            flipped = psum.tile([P, BANK], F32, tag="ta")
+            flipped = psum.tile([P, BANK], F32, tag="bank")
             for w in range(E // 2 // P):
                 nc.tensor.transpose(flipped[:, w * P : (w + 1) * P], words[:, w * P : (w + 1) * P], ident_f32[:])
             grouped = work.tile([P, E], BF16, tag="grouped", align_bytes=64)
@@ -204,7 +202,7 @@ def tile_lineartransformerblock_pc_kernel(tc, q_feat, vk, k_sum, Wo, bo, out):
             b, j = divmod(u, CHUNKS)
             rows = out[b].rearrange("(p j) c -> p j c", j=CHUNKS)
             for half in range(C_HALVES):
-                acc = psum.tile([P, BANK], F32, tag="acc", bufs=3)
+                acc = psum.tile([P, BANK], F32, tag="bank")
                 for g in range(PASSES):
                     tokens = slice(g * P, (g + 1) * P)
                     cols = slice(g * C + half * BANK, g * C + (half + 1) * BANK)
@@ -225,12 +223,16 @@ def tile_lineartransformerblock_pc_kernel(tc, q_feat, vk, k_sum, Wo, bo, out):
         READ_LAG = 1
         FLIP_LAG = 3
         PROJECT_LAG = 5
+        BIAS_STEP = 1
+        WO_STEP = 2
         for t in range(UNITS + PROJECT_LAG):
             if t < UNITS and t % CHUNKS == 0:
                 transpose_vk(t // CHUNKS)
-            if t == CHUNKS:
+            if t == BIAS_STEP:
                 spread_bias()
-                prepare_wo()
+            if 0 <= t - WO_STEP < C_HALVES * PASSES:
+                half, g = divmod(t - WO_STEP, PASSES)
+                prepare_wo(half, g)
             if t < UNITS:
                 transpose_q(t)
             if 0 <= t - FLIP_LAG < UNITS:

@@ -49,11 +49,10 @@ def tile_lineartransformerblock_pc_kernel(tc, q_feat, vk, k_sum, Wo, bo, out):
         wo_sb = keep.tile([P, C // P, E], BF16)
 
         def load_batch(b):
-            nc.sync.dma_start(out=vk_sb[b][:], in_=vk[b].rearrange("h n d -> n h d"))
             nc.sync.dma_start(out=q_sb[b][:], in_=q_feat[b].rearrange("h (p j) d -> p h (j d)", j=CHUNKS))
+            nc.sync.dma_start(out=vk_sb[b][:], in_=vk[b].rearrange("h n d -> n h d"))
 
         ks_rows = keep.tile([P, D], BF16)
-        nc.sync.dma_start(out=ks_rows[0 : B * H, :], in_=k_sum.rearrange("b h d -> (b h) d"))
         nc.vector.memset(ks_rows[32:64, :], 0.0)
         nc.vector.memset(ks_rows[64:128, :], 0.0)
         bo_rows = keep.tile([P, C], BF16)
@@ -61,6 +60,7 @@ def tile_lineartransformerblock_pc_kernel(tc, q_feat, vk, k_sum, Wo, bo, out):
 
         wo_rows = Wo.rearrange("(k p) e -> p k e", p=P)
         load_batch(0)
+        nc.sync.dma_start(out=ks_rows[0 : B * H, :], in_=k_sum.rearrange("b h d -> (b h) d"))
         nc.sync.dma_start(out=bo_rows[0:1, :], in_=bo.rearrange("(o c) -> o c", o=1))
         for half in range(C_HALVES):
             rows = slice(half * (BANK // P), (half + 1) * (BANK // P))
@@ -85,9 +85,11 @@ def tile_lineartransformerblock_pc_kernel(tc, q_feat, vk, k_sum, Wo, bo, out):
                 nc.vector.tensor_copy(out=bias[:, cols], in_=spread[:])
 
         vkT = keep.tile([P, B * H, VK_SLOT], BF16)
-        ksT = psum.tile([P, P], BF16, tag="bank")
-        nc.tensor.transpose(ksT[:], ks_rows[:], ident_bf[:])
-        nc.vector.tensor_copy(out=vkT[:, :, D : D + 1], in_=ksT[:, 0 : B * H].unsqueeze(2))
+
+        def transpose_k_sum():
+            ksT = psum.tile([P, P], BF16, tag="bank")
+            nc.tensor.transpose(ksT[:], ks_rows[:], ident_bf[:])
+            nc.vector.tensor_copy(out=vkT[:, :, D : D + 1], in_=ksT[:, 0 : B * H].unsqueeze(2))
 
         def transpose_vk(b):
             flipped = psum.tile([P, H, D], BF16, tag="bank")
@@ -192,8 +194,8 @@ def tile_lineartransformerblock_pc_kernel(tc, q_feat, vk, k_sum, Wo, bo, out):
             a_grouped[u] = grouped
 
         def quantise_a(u):
-            codes = work.tile([P, PASSES * P], U32, tag="codes", bufs=4, align_bytes=64)
-            scales = work.tile([P, PASSES * P], U8, tag="scales", bufs=4, align_bytes=64)
+            codes = work.tile([P, PASSES * P], U32, tag="codes", bufs=6, align_bytes=64)
+            scales = work.tile([P, PASSES * P], U8, tag="scales", bufs=6, align_bytes=64)
             nc.vector.quantize_mx(out=codes[:].bitcast(FP8X4), scales=scales[:], in_=a_grouped[u][:])
             a_codes[u] = codes
             a_scales[u] = scales
@@ -225,9 +227,8 @@ def tile_lineartransformerblock_pc_kernel(tc, q_feat, vk, k_sum, Wo, bo, out):
         PROJECT_LAG = 5
         BIAS_STEP = 1
         WO_STEP = 2
+        PROJECT_RUN = 2
         for t in range(UNITS + PROJECT_LAG):
-            if t < UNITS and t % CHUNKS == 0:
-                transpose_vk(t // CHUNKS)
             if t == BIAS_STEP:
                 spread_bias()
             if 0 <= t - WO_STEP < C_HALVES * PASSES:
@@ -235,11 +236,17 @@ def tile_lineartransformerblock_pc_kernel(tc, q_feat, vk, k_sum, Wo, bo, out):
                 prepare_wo(half, g)
             if t < UNITS:
                 transpose_q(t)
+            if t == 0:
+                transpose_k_sum()
+            if t < UNITS and t % CHUNKS == 0:
+                transpose_vk(t // CHUNKS)
             if 0 <= t - FLIP_LAG < UNITS:
                 transpose_a(t - FLIP_LAG)
             if 0 <= t - READ_LAG < UNITS:
                 read_out(t - READ_LAG)
             if 0 <= t - FLIP_LAG < UNITS:
                 quantise_a(t - FLIP_LAG)
-            if 0 <= t - PROJECT_LAG < UNITS:
-                project(t - PROJECT_LAG)
+            last = t - PROJECT_LAG
+            if 0 <= last < UNITS and last % PROJECT_RUN == PROJECT_RUN - 1:
+                for u in range(last - PROJECT_RUN + 1, last + 1):
+                    project(u)

@@ -17,18 +17,24 @@ E = H * D
 EPS = 1e-15
 P = 128
 PACK = 4
-K_PASS = P * PACK
-PASSES = E // K_PASS
+PASSES = E // (P * PACK)
 BANK = 512
+BANKS = 8
 CHUNKS = S // P
 UNITS = B * CHUNKS
 C_HALVES = C // BANK
+WORDS = E // 2
 READ = D + 1
 HEADS_PER_BANK = BANK // READ
-HS_BANKS = -(-H // HEADS_PER_BANK)
+READ_BANKS = -(-H // HEADS_PER_BANK)
 VK_SLOT = 144
 
-FLOPS = 2 * B * S * E * C + 2 * B * H * S * D * (D + 1)
+READ_LAG = 1
+FLIP_LAG = 3
+PROJECT_LAG = 5
+WO_STEP = 2
+
+FLOPS = 2 * B * S * E * C + 2 * B * H * S * D * READ
 
 
 def tile_lineartransformerblock_pc_kernel(tc, q_feat, vk, k_sum, Wo, bo, out):
@@ -37,36 +43,41 @@ def tile_lineartransformerblock_pc_kernel(tc, q_feat, vk, k_sum, Wo, bo, out):
         ctx.enter_context(tc.manual_schedule())
         keep = ctx.enter_context(tc.tile_pool(name="keep", bufs=1))
         work = ctx.enter_context(tc.tile_pool(name="work", bufs=3))
-        psum = ctx.enter_context(tc.psum_pool(name="psum", bufs=8))
+        psum = ctx.enter_context(tc.psum_pool(name="psum", bufs=BANKS))
 
-        vk_sb = []
         q_sb = []
+        vk_sb = []
         for b in range(B):
+            q_b = keep.tile([P, H, CHUNKS, D], BF16, name="q%d" % b)
             vk_b = keep.tile([P, H, D], BF16, name="vk%d" % b)
-            q_b = keep.tile([P, H, CHUNKS * D], BF16, name="q%d" % b)
-            vk_sb.append(vk_b)
             q_sb.append(q_b)
+            vk_sb.append(vk_b)
         wo_sb = keep.tile([P, C // P, E], BF16)
-
-        def load_batch(b):
-            nc.sync.dma_start(out=q_sb[b][:], in_=q_feat[b].rearrange("h (p j) d -> p h (j d)", j=CHUNKS))
-            nc.sync.dma_start(out=vk_sb[b][:], in_=vk[b].rearrange("h n d -> n h d"))
-
         ks_rows = keep.tile([P, D], BF16)
-        nc.vector.memset(ks_rows[32:64, :], 0.0)
-        nc.vector.memset(ks_rows[64:128, :], 0.0)
+        nc.vector.memset(ks_rows[B * H : 2 * B * H, :], 0.0)
+        nc.vector.memset(ks_rows[2 * B * H : P, :], 0.0)
         bo_rows = keep.tile([P, C], BF16)
         nc.vector.memset(bo_rows[:], 0.0)
 
-        wo_rows = Wo.rearrange("(k p) e -> p k e", p=P)
-        load_batch(0)
+        def load_q(b, first, last):
+            chunks = q_feat[b].rearrange("h (p j) d -> p h j d", j=CHUNKS)
+            nc.sync.dma_start(out=q_sb[b][:, :, first:last, :], in_=chunks[:, :, first:last, :])
+
+        def load_vk(b):
+            nc.sync.dma_start(out=vk_sb[b][:], in_=vk[b].rearrange("h n d -> n h d"))
+
+        load_q(0, 0, 1)
+        load_vk(0)
         nc.sync.dma_start(out=ks_rows[0 : B * H, :], in_=k_sum.rearrange("b h d -> (b h) d"))
         nc.sync.dma_start(out=bo_rows[0:1, :], in_=bo.rearrange("(o c) -> o c", o=1))
+        load_q(0, 1, CHUNKS)
+        wo_rows = Wo.rearrange("(k p) e -> p k e", p=P)
         for half in range(C_HALVES):
             rows = slice(half * (BANK // P), (half + 1) * (BANK // P))
             nc.sync.dma_start(out=wo_sb[:, rows, :], in_=wo_rows[:, rows, :])
         for b in range(1, B):
-            load_batch(b)
+            load_q(b, 0, CHUNKS)
+            load_vk(b)
 
         ident_bf = keep.tile([P, P], BF16)
         make_identity(nc, ident_bf[:])
@@ -87,9 +98,9 @@ def tile_lineartransformerblock_pc_kernel(tc, q_feat, vk, k_sum, Wo, bo, out):
         vkT = keep.tile([P, B * H, VK_SLOT], BF16)
 
         def transpose_k_sum():
-            ksT = psum.tile([P, P], BF16, tag="bank")
-            nc.tensor.transpose(ksT[:], ks_rows[:], ident_bf[:])
-            nc.vector.tensor_copy(out=vkT[:, :, D : D + 1], in_=ksT[:, 0 : B * H].unsqueeze(2))
+            flipped = psum.tile([P, P], BF16, tag="bank")
+            nc.tensor.transpose(flipped[:], ks_rows[:], ident_bf[:])
+            nc.vector.tensor_copy(out=vkT[:, :, D:READ], in_=flipped[:, 0 : B * H].unsqueeze(2))
 
         def transpose_vk(b):
             flipped = psum.tile([P, H, D], BF16, tag="bank")
@@ -109,7 +120,7 @@ def tile_lineartransformerblock_pc_kernel(tc, q_feat, vk, k_sum, Wo, bo, out):
                 flipped = psum.tile([P, 2, 2 * P], F32, tag="bank")
                 for u in range(2):
                     for k in range(2):
-                        first = (c0 // P + k) * (E // 2) + (2 * g + u) * P
+                        first = (c0 // P + k) * WORDS + (2 * g + u) * P
                         nc.tensor.transpose(
                             flipped[:, u, k * P : (k + 1) * P], wo_words[:, first : first + P], ident_f32[:]
                         )
@@ -135,7 +146,7 @@ def tile_lineartransformerblock_pc_kernel(tc, q_feat, vk, k_sum, Wo, bo, out):
             b, j = divmod(u, CHUNKS)
             flipped = psum.tile([P, H, P], BF16, tag="bank")
             for h in range(H):
-                nc.tensor.transpose(flipped[:, h, :], q_sb[b][:, h, j * D : (j + 1) * D], ident_bf[:])
+                nc.tensor.transpose(flipped[:, h, :], q_sb[b][:, h, j, :], ident_bf[:])
             qT_u = work.tile([P, H, P], BF16, tag="qT")
             nc.scalar.copy(out=qT_u[:], in_=flipped[:])
             qT[u] = qT_u
@@ -143,7 +154,7 @@ def tile_lineartransformerblock_pc_kernel(tc, q_feat, vk, k_sum, Wo, bo, out):
         def read_out(u):
             b = u // CHUNKS
             banks = []
-            for k in range(HS_BANKS):
+            for k in range(READ_BANKS):
                 bank = psum.tile([P, BANK], F32, tag="bank")
                 banks.append(bank)
             for h in range(H):
@@ -156,11 +167,13 @@ def tile_lineartransformerblock_pc_kernel(tc, q_feat, vk, k_sum, Wo, bo, out):
                     stop=True,
                 )
             den = work.tile([P, H], F32, tag="den")
-            for k in range(HS_BANKS):
+            for k in range(READ_BANKS):
                 h0 = k * HEADS_PER_BANK
-                n = min(HEADS_PER_BANK, H - h0)
-                slots = banks[k][:, 0 : n * READ].rearrange("p (k r) -> p k r", r=READ)
-                nc.vector.tensor_scalar_add(out=den[:, h0 : h0 + n].unsqueeze(2), in0=slots[:, :, D:READ], scalar1=EPS)
+                heads = min(HEADS_PER_BANK, H - h0)
+                slots = banks[k][:, 0 : heads * READ].rearrange("p (k r) -> p k r", r=READ)
+                nc.vector.tensor_scalar_add(
+                    out=den[:, h0 : h0 + heads].unsqueeze(2), in0=slots[:, :, D:READ], scalar1=EPS
+                )
             rden = work.tile([P, H], F32, tag="rden")
             nc.vector.reciprocal(out=rden[:], in_=den[:])
             a_u = work.tile([P, E], BF16, tag="a")
@@ -184,7 +197,7 @@ def tile_lineartransformerblock_pc_kernel(tc, q_feat, vk, k_sum, Wo, bo, out):
         def transpose_a(u):
             words = a_rows[u][:].bitcast(F32)
             flipped = psum.tile([P, BANK], F32, tag="bank")
-            for w in range(E // 2 // P):
+            for w in range(WORDS // P):
                 nc.tensor.transpose(flipped[:, w * P : (w + 1) * P], words[:, w * P : (w + 1) * P], ident_f32[:])
             grouped = work.tile([P, E], BF16, tag="grouped", align_bytes=64)
             nc.scalar.copy(
@@ -194,8 +207,8 @@ def tile_lineartransformerblock_pc_kernel(tc, q_feat, vk, k_sum, Wo, bo, out):
             a_grouped[u] = grouped
 
         def quantise_a(u):
-            codes = work.tile([P, PASSES * P], U32, tag="codes", bufs=6, align_bytes=64)
-            scales = work.tile([P, PASSES * P], U8, tag="scales", bufs=6, align_bytes=64)
+            codes = work.tile([P, PASSES * P], U32, tag="codes", bufs=4, align_bytes=64)
+            scales = work.tile([P, PASSES * P], U8, tag="scales", bufs=4, align_bytes=64)
             nc.vector.quantize_mx(out=codes[:].bitcast(FP8X4), scales=scales[:], in_=a_grouped[u][:])
             a_codes[u] = codes
             a_scales[u] = scales
@@ -222,15 +235,7 @@ def tile_lineartransformerblock_pc_kernel(tc, q_feat, vk, k_sum, Wo, bo, out):
                 nc.vector.tensor_tensor(out=res[:], in0=acc[:], in1=bias[:, cols], op=ADD)
                 nc.sync.dma_start(out=rows[:, j, cols], in_=res[:])
 
-        READ_LAG = 1
-        FLIP_LAG = 3
-        PROJECT_LAG = 5
-        BIAS_STEP = 1
-        WO_STEP = 2
-        PROJECT_RUN = 2
         for t in range(UNITS + PROJECT_LAG):
-            if t == BIAS_STEP:
-                spread_bias()
             if 0 <= t - WO_STEP < C_HALVES * PASSES:
                 half, g = divmod(t - WO_STEP, PASSES)
                 prepare_wo(half, g)
@@ -240,13 +245,13 @@ def tile_lineartransformerblock_pc_kernel(tc, q_feat, vk, k_sum, Wo, bo, out):
                 transpose_k_sum()
             if t < UNITS and t % CHUNKS == 0:
                 transpose_vk(t // CHUNKS)
+            if t == 0:
+                spread_bias()
             if 0 <= t - FLIP_LAG < UNITS:
                 transpose_a(t - FLIP_LAG)
             if 0 <= t - READ_LAG < UNITS:
                 read_out(t - READ_LAG)
             if 0 <= t - FLIP_LAG < UNITS:
                 quantise_a(t - FLIP_LAG)
-            last = t - PROJECT_LAG
-            if 0 <= last < UNITS and last % PROJECT_RUN == PROJECT_RUN - 1:
-                for u in range(last - PROJECT_RUN + 1, last + 1):
-                    project(u)
+            if 0 <= t - PROJECT_LAG < UNITS:
+                project(t - PROJECT_LAG)

from contextlib import ExitStack

import concourse.mybir as mybir
from concourse.masks import make_identity

BF16 = mybir.dt.bfloat16
F32 = mybir.dt.float32
U32 = mybir.dt.uint32
U8 = mybir.dt.uint8
FP8X4 = mybir.dt.float8_e4m3fn_x4
COPY = mybir.ActivationFunctionType.Copy
ADD = mybir.AluOpType.add
MULT = mybir.AluOpType.mult

B, H, S, D, C = 4, 8, 512, 128, 1024
E = H * D
EPS = 1e-15
P = 128
PACK = 4
PASSES = E // (P * PACK)
BANK = 512
BANKS = 8
CHUNKS = S // P
UNITS = B * CHUNKS
C_HALVES = C // BANK
WORDS = E // 2
READ = D + 1
HEADS_PER_BANK = BANK // READ
READ_BANKS = -(-H // HEADS_PER_BANK)
VK_SLOT = 144

READ_LAG = 1
FLIP_LAG = 3
PROJECT_LAG = 5
WO_STEP = 2

FLOPS = 2 * B * S * E * C + 2 * B * H * S * D * READ


def tile_lineartransformerblock_pc_kernel(tc, q_feat, vk, k_sum, Wo, bo, out):
    nc = tc.nc
    with ExitStack() as ctx:
        ctx.enter_context(tc.manual_schedule())
        keep = ctx.enter_context(tc.tile_pool(name="keep", bufs=1))
        work = ctx.enter_context(tc.tile_pool(name="work", bufs=3))
        psum = ctx.enter_context(tc.psum_pool(name="psum", bufs=BANKS))

        q_sb = []
        vk_sb = []
        for b in range(B):
            q_b = keep.tile([P, H, CHUNKS, D], BF16, name="q%d" % b)
            vk_b = keep.tile([P, H, D], BF16, name="vk%d" % b)
            q_sb.append(q_b)
            vk_sb.append(vk_b)
        wo_sb = keep.tile([P, C // P, E], BF16)
        ks_rows = keep.tile([P, D], BF16)
        nc.vector.memset(ks_rows[B * H : 2 * B * H, :], 0.0)
        nc.vector.memset(ks_rows[2 * B * H : P, :], 0.0)
        bo_rows = keep.tile([P, C], BF16)
        nc.vector.memset(bo_rows[:], 0.0)

        def load_q(b, first, last):
            chunks = q_feat[b].rearrange("h (p j) d -> p h j d", j=CHUNKS)
            nc.sync.dma_start(out=q_sb[b][:, :, first:last, :], in_=chunks[:, :, first:last, :])

        def load_vk(b):
            nc.sync.dma_start(out=vk_sb[b][:], in_=vk[b].rearrange("h n d -> n h d"))

        load_q(0, 0, 1)
        load_vk(0)
        nc.sync.dma_start(out=ks_rows[0 : B * H, :], in_=k_sum.rearrange("b h d -> (b h) d"))
        nc.sync.dma_start(out=bo_rows[0:1, :], in_=bo.rearrange("(o c) -> o c", o=1))
        load_q(0, 1, CHUNKS)
        wo_rows = Wo.rearrange("(k p) e -> p k e", p=P)
        for half in range(C_HALVES):
            rows = slice(half * (BANK // P), (half + 1) * (BANK // P))
            nc.sync.dma_start(out=wo_sb[:, rows, :], in_=wo_rows[:, rows, :])
        for b in range(1, B):
            load_q(b, 0, CHUNKS)
            load_vk(b)

        ident_bf = keep.tile([P, P], BF16)
        make_identity(nc, ident_bf[:])
        ident_f32 = keep.tile([P, P], F32)
        make_identity(nc, ident_f32[:])
        ones = keep.tile([P, P], BF16)
        nc.vector.memset(ones[:], 1.0)

        bias = keep.tile([P, C], F32)

        def spread_bias():
            for half in range(C_HALVES):
                cols = slice(half * BANK, (half + 1) * BANK)
                spread = psum.tile([P, BANK], F32, tag="bank")
                nc.tensor.matmul(out=spread[:], lhsT=ones[:], rhs=bo_rows[:, cols], start=True, stop=True)
                nc.vector.tensor_copy(out=bias[:, cols], in_=spread[:])

        vkT = keep.tile([P, B * H, VK_SLOT], BF16)

        def transpose_k_sum():
            flipped = psum.tile([P, P], BF16, tag="bank")
            nc.tensor.transpose(flipped[:], ks_rows[:], ident_bf[:])
            nc.vector.tensor_copy(out=vkT[:, :, D:READ], in_=flipped[:, 0 : B * H].unsqueeze(2))

        def transpose_vk(b):
            flipped = psum.tile([P, H, D], BF16, tag="bank")
            for h in range(H):
                nc.tensor.transpose(flipped[:, h, :], vk_sb[b][:, h, :], ident_bf[:])
            nc.vector.tensor_copy(out=vkT[:, b * H : (b + 1) * H, 0:D], in_=flipped[:])

        wo_words = wo_sb[:].rearrange("p k e -> p (k e)").bitcast(F32)
        wo_grouped = keep.tile([P, PASSES * C * PACK], BF16, align_bytes=64)
        wo_pairs = wo_grouped[:].bitcast(F32).rearrange("p (g c u) -> p g c u", g=PASSES, u=2)
        wo_codes = keep.tile([P, PASSES * C], U32, align_bytes=64)
        wo_scales = keep.tile([P, PASSES * C], U8, align_bytes=64)

        def prepare_wo(half, g):
            for quarter in range(2):
                c0 = half * BANK + quarter * 2 * P
                flipped = psum.tile([P, 2, 2 * P], F32, tag="bank")
                for u in range(2):
                    for k in range(2):
                        first = (c0 // P + k) * WORDS + (2 * g + u) * P
                        nc.tensor.transpose(
                            flipped[:, u, k * P : (k + 1) * P], wo_words[:, first : first + P], ident_f32[:]
                        )
                pairs = wo_pairs[:, g, c0 : c0 + 2 * P, :]
                if quarter == 0:
                    nc.scalar.copy(out=pairs, in_=flipped[:].rearrange("p u c -> p c u"))
                else:
                    nc.vector.tensor_copy(out=pairs, in_=flipped[:].rearrange("p u c -> p c u"))
            first = g * C + half * BANK
            nc.vector.quantize_mx(
                out=wo_codes[:, first : first + BANK].bitcast(FP8X4),
                scales=wo_scales[:, first : first + BANK],
                in_=wo_grouped[:, first * PACK : (first + BANK) * PACK],
            )

        qT = {}
        a_rows = {}
        a_grouped = {}
        a_codes = {}
        a_scales = {}

        def transpose_q(u):
            b, j = divmod(u, CHUNKS)
            flipped = psum.tile([P, H, P], BF16, tag="bank")
            for h in range(H):
                nc.tensor.transpose(flipped[:, h, :], q_sb[b][:, h, j, :], ident_bf[:])
            qT_u = work.tile([P, H, P], BF16, tag="qT")
            nc.scalar.copy(out=qT_u[:], in_=flipped[:])
            qT[u] = qT_u

        def read_out(u):
            b = u // CHUNKS
            banks = []
            for k in range(READ_BANKS):
                bank = psum.tile([P, BANK], F32, tag="bank")
                banks.append(bank)
            for h in range(H):
                k, slot = divmod(h, HEADS_PER_BANK)
                nc.tensor.matmul(
                    out=banks[k][:, slot * READ : (slot + 1) * READ],
                    lhsT=qT[u][:, h, :],
                    rhs=vkT[:, b * H + h, 0:READ],
                    start=True,
                    stop=True,
                )
            den = work.tile([P, H], F32, tag="den")
            for k in range(READ_BANKS):
                h0 = k * HEADS_PER_BANK
                heads = min(HEADS_PER_BANK, H - h0)
                slots = banks[k][:, 0 : heads * READ].rearrange("p (k r) -> p k r", r=READ)
                nc.vector.tensor_scalar_add(
                    out=den[:, h0 : h0 + heads].unsqueeze(2), in0=slots[:, :, D:READ], scalar1=EPS
                )
            rden = work.tile([P, H], F32, tag="rden")
            nc.vector.reciprocal(out=rden[:], in_=den[:])
            a_u = work.tile([P, E], BF16, tag="a")
            first_heads = banks[0][:, 0 : HEADS_PER_BANK * READ].rearrange("p (k r) -> p k r", r=READ)
            nc.vector.tensor_tensor(
                out=a_u[:, 0 : HEADS_PER_BANK * D].rearrange("p (k n) -> p k n", n=D),
                in0=first_heads[:, :, 0:D],
                in1=rden[:, 0:HEADS_PER_BANK].unsqueeze(2).to_broadcast([P, HEADS_PER_BANK, D]),
                op=MULT,
            )
            for h in range(HEADS_PER_BANK, H):
                k, slot = divmod(h, HEADS_PER_BANK)
                nc.scalar.activation(
                    out=a_u[:, h * D : (h + 1) * D],
                    in_=banks[k][:, slot * READ : slot * READ + D],
                    func=COPY,
                    scale=rden[:, h : h + 1],
                )
            a_rows[u] = a_u

        def transpose_a(u):
            words = a_rows[u][:].bitcast(F32)
            flipped = psum.tile([P, BANK], F32, tag="bank")
            for w in range(WORDS // P):
                nc.tensor.transpose(flipped[:, w * P : (w + 1) * P], words[:, w * P : (w + 1) * P], ident_f32[:])
            grouped = work.tile([P, E], BF16, tag="grouped", align_bytes=64)
            nc.scalar.copy(
                out=grouped[:].bitcast(F32).rearrange("p (g s u) -> p g s u", g=PASSES, u=2),
                in_=flipped[:].rearrange("p (g u s) -> p g s u", g=PASSES, u=2),
            )
            a_grouped[u] = grouped

        def quantise_a(u):
            codes = work.tile([P, PASSES * P], U32, tag="codes", bufs=4, align_bytes=64)
            scales = work.tile([P, PASSES * P], U8, tag="scales", bufs=4, align_bytes=64)
            nc.vector.quantize_mx(out=codes[:].bitcast(FP8X4), scales=scales[:], in_=a_grouped[u][:])
            a_codes[u] = codes
            a_scales[u] = scales

        def project(u):
            b, j = divmod(u, CHUNKS)
            rows = out[b].rearrange("(p j) c -> p j c", j=CHUNKS)
            for half in range(C_HALVES):
                acc = psum.tile([P, BANK], F32, tag="bank")
                for g in range(PASSES):
                    tokens = slice(g * P, (g + 1) * P)
                    cols = slice(g * C + half * BANK, g * C + (half + 1) * BANK)
                    nc.tensor.matmul_mx(
                        out=acc[:],
                        lhsT=a_codes[u][:, tokens].bitcast(FP8X4),
                        lhsT_scale=a_scales[u][:, tokens],
                        rhs=wo_codes[:, cols].bitcast(FP8X4),
                        rhs_scale=wo_scales[:, cols],
                        start=(g == 0),
                        stop=(g == PASSES - 1),
                    )
                cols = slice(half * BANK, (half + 1) * BANK)
                res = work.tile([P, BANK], F32, tag="res", bufs=6)
                nc.vector.tensor_tensor(out=res[:], in0=acc[:], in1=bias[:, cols], op=ADD)
                nc.sync.dma_start(out=rows[:, j, cols], in_=res[:])

        for t in range(UNITS + PROJECT_LAG):
            if 0 <= t - WO_STEP < C_HALVES * PASSES:
                half, g = divmod(t - WO_STEP, PASSES)
                prepare_wo(half, g)
            if t < UNITS:
                transpose_q(t)
            if t == 0:
                transpose_k_sum()
            if t < UNITS and t % CHUNKS == 0:
                transpose_vk(t // CHUNKS)
            if t == 0:
                spread_bias()
            if 0 <= t - FLIP_LAG < UNITS:
                transpose_a(t - FLIP_LAG)
            if 0 <= t - READ_LAG < UNITS:
                read_out(t - READ_LAG)
            if 0 <= t - FLIP_LAG < UNITS:
                quantise_a(t - FLIP_LAG)
            if 0 <= t - PROJECT_LAG < UNITS:
                project(t - PROJECT_LAG)
